import numpy as np
import ml_dtypes

BF16 = ml_dtypes.bfloat16


def bf(x):
    return np.asarray(x, np.float32).astype(BF16)


def f32(x):
    return np.asarray(x, np.float32)


def f64(x):
    return np.asarray(x).astype(np.float64)


def striped(idx):
    return np.tile(idx.reshape(-1, 16).T, (8, 1))


D, S, E, NC, M, N = 128, 1024, 4, 128, 512, 1024
LENGTH_SCALE = 0.1


def setup_inputs():
    return {"table": bf(np.random.standard_normal((D, S))), "w": bf(0.15 * np.random.standard_normal((D, M)) / np.sqrt(D)), "csum": f32(0.2 * np.random.standard_normal((NC, E))), "cnum": f32(1.0 + np.random.uniform(size=(NC, 1))), "offs": striped(np.random.permutation(np.tile(np.arange(S), 2))[:N])}


def reference(table, w, csum, cnum, offs):
    idx = offs[:16].T.reshape(-1)
    z = (f64(w).T @ f64(table)[:, idx]).reshape(E, NC, N)
    cen = (f64(csum) / f64(cnum)).T[:, :, None]
    sq = np.mean((z - cen) ** 2, axis=0)
    return np.exp(-sq / (2.0 * LENGTH_SCALE ** 2))

@@ -1,0 +1,57 @@
+import concourse.mybir as mybir
+
+BF16, F32, U16 = mybir.dt.bfloat16, mybir.dt.float32, mybir.dt.uint16
+SQUARE = mybir.ActivationFunctionType.Square
+EXP = mybir.ActivationFunctionType.Exp
+MULT = mybir.AluOpType.mult
+
+P = 128
+S = 1024
+E = 4
+N = 1024
+PIECE = 512
+LENGTH_SCALE = 0.1
+
+FLOPS = 2 * P * (E * P) * N
+
+
+def tile_duqclassifier_kernel(tc, table, w, csum, cnum, offs, out):
+    nc = tc.nc
+    with (
+        tc.tile_pool(name="held", bufs=1) as held,
+        tc.tile_pool(name="work", bufs=2) as work,
+        tc.psum_pool(name="psum", bufs=8) as psum,
+    ):
+        offsets = held.tile([P, N // 16], U16, name="offsets")
+        nc.sync.dma_start(offsets[:], offs)
+        store = held.tile([P, S], BF16, name="store")
+        nc.scalar.dma_start(store[:], table)
+        weights = held.tile([P, E * P], BF16, name="weights")
+        nc.gpsimd.dma_start(weights[:], w)
+        sums = held.tile([P, E], F32, name="sums")
+        nc.sync.dma_start(sums[:], csum)
+        counts = held.tile([P, 1], F32, name="counts")
+        nc.sync.dma_start(counts[:], cnum)
+
+        inv_counts = held.tile([P, 1], F32, name="inv_counts")
+        nc.vector.reciprocal(inv_counts[:], counts[:])
+        neg_cen = held.tile([P, E], F32, name="neg_cen")
+        nc.vector.tensor_scalar(neg_cen[:], sums[:], inv_counts[:, 0:1], -1.0, MULT, MULT)
+
+        for piece in range(N // PIECE):
+            picked = store[:].indirect(
+                offsets[:, piece * (PIECE // 16) : (piece + 1) * (PIECE // 16)]
+            )
+            total = work.tile([P, PIECE], F32, name="total")
+            for e in range(E):
+                z = psum.tile([P, PIECE], F32, name="z")
+                nc.tensor.matmul(z[:], weights[:, e * P : (e + 1) * P], picked, start=True, stop=True)
+                if e == 0:
+                    nc.scalar.activation(total[:], z[:], SQUARE, bias=neg_cen[:, e : e + 1])
+                else:
+                    sq = work.tile([P, PIECE], F32, name="sq")
+                    nc.scalar.activation(sq[:], z[:], SQUARE, bias=neg_cen[:, e : e + 1])
+                    nc.vector.tensor_add(total[:], total[:], sq[:])
+            conf = work.tile([P, PIECE], F32, name="conf")
+            nc.scalar.activation(conf[:], total[:], EXP, scale=-1.0 / (E * 2.0 * LENGTH_SCALE**2))
+            nc.sync.dma_start(out[:, piece * PIECE : (piece + 1) * PIECE], conf[:])

@@ -19,26 +19,30 @@ def tile_duqclassifier_kernel(tc, table, w, csum, cnum, offs, out):
     nc = tc.nc
     with (
         tc.tile_pool(name="held", bufs=1) as held,
-        tc.tile_pool(name="work", bufs=2) as work,
+        tc.tile_pool(name="work", bufs=3) as work,
         tc.psum_pool(name="psum", bufs=8) as psum,
     ):
         offsets = held.tile([P, N // 16], U16, name="offsets")
         nc.sync.dma_start(offsets[:], offs)
         store = held.tile([P, S], BF16, name="store")
-        nc.scalar.dma_start(store[:], table)
+        nc.sync.dma_start(store[:], table)
         weights = held.tile([P, E * P], BF16, name="weights")
-        nc.gpsimd.dma_start(weights[:], w)
+        nc.scalar.dma_start(weights[:], w)
         sums = held.tile([P, E], F32, name="sums")
-        nc.sync.dma_start(sums[:], csum)
+        nc.scalar.dma_start(sums[:], csum)
         counts = held.tile([P, 1], F32, name="counts")
-        nc.sync.dma_start(counts[:], cnum)
+        nc.scalar.dma_start(counts[:], cnum)
+
+        scratch = held.tile([P, 1], F32, name="scratch")
+        nc.vector.memset(scratch[:], 0.0)
+        nc.scalar.activation(scratch[:], scratch[:], EXP)
 
         inv_counts = held.tile([P, 1], F32, name="inv_counts")
         nc.vector.reciprocal(inv_counts[:], counts[:])
         neg_cen = held.tile([P, E], F32, name="neg_cen")
         nc.vector.tensor_scalar(neg_cen[:], sums[:], inv_counts[:, 0:1], -1.0, MULT, MULT)
 
-        for piece in range(N // PIECE):
+        def distances(piece):
             picked = store[:].indirect(
                 offsets[:, piece * (PIECE // 16) : (piece + 1) * (PIECE // 16)]
             )
@@ -52,6 +56,16 @@ def tile_duqclassifier_kernel(tc, table, w, csum, cnum, offs, out):
                     sq = work.tile([P, PIECE], F32, name="sq")
                     nc.scalar.activation(sq[:], z[:], SQUARE, bias=neg_cen[:, e : e + 1])
                     nc.vector.tensor_add(total[:], total[:], sq[:])
+            return total
+
+        def confidences(piece, total):
             conf = work.tile([P, PIECE], F32, name="conf")
             nc.scalar.activation(conf[:], total[:], EXP, scale=-1.0 / (E * 2.0 * LENGTH_SCALE**2))
             nc.sync.dma_start(out[:, piece * PIECE : (piece + 1) * PIECE], conf[:])
+
+        pieces = N // PIECE
+        totals = [distances(0)]
+        for piece in range(1, pieces):
+            totals.append(distances(piece))
+            confidences(piece - 1, totals[piece - 1])
+        confidences(pieces - 1, totals[pieces - 1])

@@ -9,7 +9,7 @@ P = 128
 S = 1024
 E = 4
 N = 1024
-PIECE = 512
+PIECE = 256
 LENGTH_SCALE = 0.1
 
 FLOPS = 2 * P * (E * P) * N

@@ -9,7 +9,8 @@ P = 128
 S = 1024
 E = 4
 N = 1024
-PIECE = 256
+PIECE = 512
+WARMUP = 6
 LENGTH_SCALE = 0.1
 
 FLOPS = 2 * P * (E * P) * N
@@ -25,13 +26,19 @@ def tile_duqclassifier_kernel(tc, table, w, csum, cnum, offs, out):
         offsets = held.tile([P, N // 16], U16, name="offsets")
         nc.sync.dma_start(offsets[:], offs)
         store = held.tile([P, S], BF16, name="store")
-        nc.sync.dma_start(store[:], table)
         weights = held.tile([P, E * P], BF16, name="weights")
+        nc.sync.dma_start(store[:], table)
         nc.scalar.dma_start(weights[:], w)
         sums = held.tile([P, E], F32, name="sums")
         nc.scalar.dma_start(sums[:], csum)
         counts = held.tile([P, 1], F32, name="counts")
         nc.scalar.dma_start(counts[:], cnum)
+
+        zeros = held.tile([P, PIECE], BF16, name="zeros")
+        nc.vector.memset(zeros[:], 0.0)
+        unread = psum.tile([P, PIECE], F32, name="unread", tag="z")
+        for _ in range(WARMUP):
+            nc.tensor.matmul(unread[:], zeros[:, 0:P], zeros[:], start=True, stop=True)
 
         scratch = held.tile([P, 1], F32, name="scratch")
         nc.vector.memset(scratch[:], 0.0)

@@ -10,7 +10,7 @@ S = 1024
 E = 4
 N = 1024
 PIECE = 512
-WARMUP = 6
+ROW_BYTES = 512
 LENGTH_SCALE = 0.1
 
 FLOPS = 2 * P * (E * P) * N
@@ -18,6 +18,11 @@ FLOPS = 2 * P * (E * P) * N
 
 def tile_duqclassifier_kernel(tc, table, w, csum, cnum, offs, out):
     nc = tc.nc
+
+    def move_in_blocks(queue, target, source, block):
+        for first in range(0, target.shape[1], block):
+            queue.dma_start(target[:, first : first + block], source[:, first : first + block])
+
     with (
         tc.tile_pool(name="held", bufs=1) as held,
         tc.tile_pool(name="work", bufs=3) as work,
@@ -26,19 +31,13 @@ def tile_duqclassifier_kernel(tc, table, w, csum, cnum, offs, out):
         offsets = held.tile([P, N // 16], U16, name="offsets")
         nc.sync.dma_start(offsets[:], offs)
         store = held.tile([P, S], BF16, name="store")
+        move_in_blocks(nc.sync, store, table, ROW_BYTES // 2)
         weights = held.tile([P, E * P], BF16, name="weights")
-        nc.sync.dma_start(store[:], table)
-        nc.scalar.dma_start(weights[:], w)
         sums = held.tile([P, E], F32, name="sums")
-        nc.scalar.dma_start(sums[:], csum)
         counts = held.tile([P, 1], F32, name="counts")
+        move_in_blocks(nc.scalar, weights, w, ROW_BYTES // 2)
+        nc.scalar.dma_start(sums[:], csum)
         nc.scalar.dma_start(counts[:], cnum)
-
-        zeros = held.tile([P, PIECE], BF16, name="zeros")
-        nc.vector.memset(zeros[:], 0.0)
-        unread = psum.tile([P, PIECE], F32, name="unread", tag="z")
-        for _ in range(WARMUP):
-            nc.tensor.matmul(unread[:], zeros[:, 0:P], zeros[:], start=True, stop=True)
 
         scratch = held.tile([P, 1], F32, name="scratch")
         nc.vector.memset(scratch[:], 0.0)
@@ -68,7 +67,7 @@ def tile_duqclassifier_kernel(tc, table, w, csum, cnum, offs, out):
         def confidences(piece, total):
             conf = work.tile([P, PIECE], F32, name="conf")
             nc.scalar.activation(conf[:], total[:], EXP, scale=-1.0 / (E * 2.0 * LENGTH_SCALE**2))
-            nc.sync.dma_start(out[:, piece * PIECE : (piece + 1) * PIECE], conf[:])
+            move_in_blocks(nc.sync, out[:, piece * PIECE : (piece + 1) * PIECE], conf, ROW_BYTES // 4)
 
         pieces = N // PIECE
         totals = [distances(0)]

@@ -10,7 +10,7 @@ S = 1024
 E = 4
 N = 1024
 PIECE = 512
-ROW_BYTES = 512
+PIECES = N // PIECE
 LENGTH_SCALE = 0.1
 
 FLOPS = 2 * P * (E * P) * N
@@ -18,25 +18,20 @@ FLOPS = 2 * P * (E * P) * N
 
 def tile_duqclassifier_kernel(tc, table, w, csum, cnum, offs, out):
     nc = tc.nc
-
-    def move_in_blocks(queue, target, source, block):
-        for first in range(0, target.shape[1], block):
-            queue.dma_start(target[:, first : first + block], source[:, first : first + block])
-
     with (
         tc.tile_pool(name="held", bufs=1) as held,
         tc.tile_pool(name="work", bufs=3) as work,
-        tc.psum_pool(name="psum", bufs=8) as psum,
+        tc.psum_pool(name="psum", bufs=E * PIECES) as psum,
     ):
         offsets = held.tile([P, N // 16], U16, name="offsets")
         nc.sync.dma_start(offsets[:], offs)
         store = held.tile([P, S], BF16, name="store")
-        move_in_blocks(nc.sync, store, table, ROW_BYTES // 2)
+        nc.sync.dma_start(store[:], table)
         weights = held.tile([P, E * P], BF16, name="weights")
+        nc.scalar.dma_start(weights[:], w)
         sums = held.tile([P, E], F32, name="sums")
-        counts = held.tile([P, 1], F32, name="counts")
-        move_in_blocks(nc.scalar, weights, w, ROW_BYTES // 2)
         nc.scalar.dma_start(sums[:], csum)
+        counts = held.tile([P, 1], F32, name="counts")
         nc.scalar.dma_start(counts[:], cnum)
 
         scratch = held.tile([P, 1], F32, name="scratch")
@@ -48,30 +43,24 @@ def tile_duqclassifier_kernel(tc, table, w, csum, cnum, offs, out):
         neg_cen = held.tile([P, E], F32, name="neg_cen")
         nc.vector.tensor_scalar(neg_cen[:], sums[:], inv_counts[:, 0:1], -1.0, MULT, MULT)
 
-        def distances(piece):
-            picked = store[:].indirect(
-                offsets[:, piece * (PIECE // 16) : (piece + 1) * (PIECE // 16)]
-            )
-            total = work.tile([P, PIECE], F32, name="total")
-            for e in range(E):
+        totals = [held.tile([P, PIECE], F32, name=f"total{piece}") for piece in range(PIECES)]
+        for e in range(E):
+            for piece in range(PIECES):
+                picked = store[:].indirect(
+                    offsets[:, piece * (PIECE // 16) : (piece + 1) * (PIECE // 16)]
+                )
                 z = psum.tile([P, PIECE], F32, name="z")
                 nc.tensor.matmul(z[:], weights[:, e * P : (e + 1) * P], picked, start=True, stop=True)
                 if e == 0:
-                    nc.scalar.activation(total[:], z[:], SQUARE, bias=neg_cen[:, e : e + 1])
+                    nc.scalar.activation(totals[piece][:], z[:], SQUARE, bias=neg_cen[:, e : e + 1])
                 else:
                     sq = work.tile([P, PIECE], F32, name="sq")
                     nc.scalar.activation(sq[:], z[:], SQUARE, bias=neg_cen[:, e : e + 1])
-                    nc.vector.tensor_add(total[:], total[:], sq[:])
-            return total
+                    nc.vector.tensor_add(totals[piece][:], totals[piece][:], sq[:])
 
-        def confidences(piece, total):
+        for piece in range(PIECES):
             conf = work.tile([P, PIECE], F32, name="conf")
-            nc.scalar.activation(conf[:], total[:], EXP, scale=-1.0 / (E * 2.0 * LENGTH_SCALE**2))
-            move_in_blocks(nc.sync, out[:, piece * PIECE : (piece + 1) * PIECE], conf, ROW_BYTES // 4)
-
-        pieces = N // PIECE
-        totals = [distances(0)]
-        for piece in range(1, pieces):
-            totals.append(distances(piece))
-            confidences(piece - 1, totals[piece - 1])
-        confidences(pieces - 1, totals[pieces - 1])
+            nc.scalar.activation(
+                conf[:], totals[piece][:], EXP, scale=-1.0 / (E * 2.0 * LENGTH_SCALE**2)
+            )
+            nc.sync.dma_start(out[:, piece * PIECE : (piece + 1) * PIECE], conf[:])

@@ -11,6 +11,7 @@ E = 4
 N = 1024
 PIECE = 512
 PIECES = N // PIECE
+HALVES = (slice(0, PIECE // 2), slice(PIECE // 2, PIECE))
 LENGTH_SCALE = 0.1
 
 FLOPS = 2 * P * (E * P) * N
@@ -56,11 +57,18 @@ def tile_duqclassifier_kernel(tc, table, w, csum, cnum, offs, out):
                 else:
                     sq = work.tile([P, PIECE], F32, name="sq")
                     nc.scalar.activation(sq[:], z[:], SQUARE, bias=neg_cen[:, e : e + 1])
-                    nc.vector.tensor_add(totals[piece][:], totals[piece][:], sq[:])
+                    for half in HALVES if e == E - 1 else (slice(0, PIECE),):
+                        nc.vector.tensor_add(
+                            totals[piece][:, half], totals[piece][:, half], sq[:, half]
+                        )
 
         for piece in range(PIECES):
             conf = work.tile([P, PIECE], F32, name="conf")
-            nc.scalar.activation(
-                conf[:], totals[piece][:], EXP, scale=-1.0 / (E * 2.0 * LENGTH_SCALE**2)
-            )
+            for half in HALVES:
+                nc.scalar.activation(
+                    conf[:, half],
+                    totals[piece][:, half],
+                    EXP,
+                    scale=-1.0 / (E * 2.0 * LENGTH_SCALE**2),
+                )
             nc.sync.dma_start(out[:, piece * PIECE : (piece + 1) * PIECE], conf[:])

import concourse.mybir as mybir

BF16, F32, U16 = mybir.dt.bfloat16, mybir.dt.float32, mybir.dt.uint16
SQUARE = mybir.ActivationFunctionType.Square
EXP = mybir.ActivationFunctionType.Exp
MULT = mybir.AluOpType.mult

P = 128
S = 1024
E = 4
N = 1024
PIECE = 512
PIECES = N // PIECE
HALVES = (slice(0, PIECE // 2), slice(PIECE // 2, PIECE))
LENGTH_SCALE = 0.1

FLOPS = 2 * P * (E * P) * N


def tile_duqclassifier_kernel(tc, table, w, csum, cnum, offs, out):
    nc = tc.nc
    with (
        tc.tile_pool(name="held", bufs=1) as held,
        tc.tile_pool(name="work", bufs=3) as work,
        tc.psum_pool(name="psum", bufs=E * PIECES) as psum,
    ):
        offsets = held.tile([P, N // 16], U16, name="offsets")
        nc.sync.dma_start(offsets[:], offs)
        store = held.tile([P, S], BF16, name="store")
        nc.sync.dma_start(store[:], table)
        weights = held.tile([P, E * P], BF16, name="weights")
        nc.scalar.dma_start(weights[:], w)
        sums = held.tile([P, E], F32, name="sums")
        nc.scalar.dma_start(sums[:], csum)
        counts = held.tile([P, 1], F32, name="counts")
        nc.scalar.dma_start(counts[:], cnum)

        scratch = held.tile([P, 1], F32, name="scratch")
        nc.vector.memset(scratch[:], 0.0)
        nc.scalar.activation(scratch[:], scratch[:], EXP)

        inv_counts = held.tile([P, 1], F32, name="inv_counts")
        nc.vector.reciprocal(inv_counts[:], counts[:])
        neg_cen = held.tile([P, E], F32, name="neg_cen")
        nc.vector.tensor_scalar(neg_cen[:], sums[:], inv_counts[:, 0:1], -1.0, MULT, MULT)

        totals = [held.tile([P, PIECE], F32, name=f"total{piece}") for piece in range(PIECES)]
        for e in range(E):
            for piece in range(PIECES):
                picked = store[:].indirect(
                    offsets[:, piece * (PIECE // 16) : (piece + 1) * (PIECE // 16)]
                )
                z = psum.tile([P, PIECE], F32, name="z")
                nc.tensor.matmul(z[:], weights[:, e * P : (e + 1) * P], picked, start=True, stop=True)
                if e == 0:
                    nc.scalar.activation(totals[piece][:], z[:], SQUARE, bias=neg_cen[:, e : e + 1])
                else:
                    sq = work.tile([P, PIECE], F32, name="sq")
                    nc.scalar.activation(sq[:], z[:], SQUARE, bias=neg_cen[:, e : e + 1])
                    for half in HALVES if e == E - 1 else (slice(0, PIECE),):
                        nc.vector.tensor_add(
                            totals[piece][:, half], totals[piece][:, half], sq[:, half]
                        )

        for piece in range(PIECES):
            conf = work.tile([P, PIECE], F32, name="conf")
            for half in HALVES:
                nc.scalar.activation(
                    conf[:, half],
                    totals[piece][:, half],
                    EXP,
                    scale=-1.0 / (E * 2.0 * LENGTH_SCALE**2),
                )
            nc.sync.dma_start(out[:, piece * PIECE : (piece + 1) * PIECE], conf[:])
